import numpy as np
import ml_dtypes

BF16 = ml_dtypes.bfloat16


def bf(x):
    return np.asarray(x, np.float32).astype(BF16)


def f32(x):
    return np.asarray(x, np.float32)


def f64(x):
    return np.asarray(x).astype(np.float64)


def striped(idx):
    return np.tile(idx.reshape(-1, 16).T, (8, 1))


S, D, M, F, N = 2048, 128, 128, 128, 1024


def setup_inputs():
    return {"table": bf(np.random.standard_normal((S, D))), "w": bf(np.random.standard_normal((D, M)) / np.sqrt(D)), "b": f32(0.1 * np.random.standard_normal((M, 1))), "w1": bf(np.random.standard_normal((M, F)) / np.sqrt(M)), "b1": f32(0.1 * np.random.standard_normal((F, 1))), "w2": bf(np.random.standard_normal((F, M)) / np.sqrt(F)), "b2": f32(0.1 * np.random.standard_normal((M, 1))), "offs": striped(np.random.permutation(np.tile(np.arange(S), 2))[:N])}


def reference(table, w, b, w1, b1, w2, b2, offs):
    idx = offs[:16].T.reshape(-1)
    state = f64(w).T @ f64(table)[idx].T + f64(b)
    hid = np.maximum(f64(w1).T @ state + f64(b1), 0.0)
    msg = f64(w2).T @ hid + f64(b2)
    return np.concatenate([state, msg], axis=0)

@@ -1,0 +1,102 @@
+import concourse.mybir as mybir
+from concourse.masks import make_identity
+
+BF16 = mybir.dt.bfloat16
+F32 = mybir.dt.float32
+U16 = mybir.dt.uint16
+ADD = mybir.AluOpType.add
+IDENTITY = mybir.ActivationFunctionType.Identity
+RELU = mybir.ActivationFunctionType.Relu
+
+P = 128
+WORDS = 2048
+NODES = 1024
+PIECE = 256
+N_PIECES = NODES // PIECE
+OFFS_COLS = PIECE // 16
+BLOCKS = 4
+CHUNK = BLOCKS * P
+N_CHUNKS = WORDS // CHUNK
+
+FLOPS = 3 * 2 * P * P * NODES
+
+
+def tile_gpnn_kernel(tc, table, w, b, w1, b1, w2, b2, offs, out):
+    nc = tc.nc
+    table_chunks = table.rearrange("(c k p) d -> c p k d", k=BLOCKS, p=P)
+    with (
+        tc.tile_pool(name="held", bufs=1) as held,
+        tc.tile_pool(name="rows", bufs=N_CHUNKS) as rows,
+        tc.tile_pool(name="work", bufs=N_PIECES) as work,
+    ):
+        word_rows = []
+        for c in range(N_CHUNKS):
+            chunk = rows.tile([P, BLOCKS, P], BF16, name="word_rows")
+            queue = nc.sync if c % 2 == 0 else nc.scalar
+            queue.dma_start(chunk[:], table_chunks[c])
+            word_rows.append(chunk)
+
+        offsets = held.tile([P, NODES // 16], U16, name="offsets")
+        nc.sync.dma_start(offsets[:], offs)
+
+        w_sb = held.tile([P, P], BF16, name="w_sb")
+        w1_sb = held.tile([P, P], BF16, name="w1_sb")
+        w2_sb = held.tile([P, P], BF16, name="w2_sb")
+        nc.sync.dma_start(w_sb[:], w)
+        nc.scalar.dma_start(w1_sb[:], w1)
+        nc.scalar.dma_start(w2_sb[:], w2)
+
+        b_sb = held.tile([P, 1], F32, name="b_sb")
+        b1_sb = held.tile([P, 1], F32, name="b1_sb")
+        b2_sb = held.tile([P, 1], F32, name="b2_sb")
+        nc.sync.dma_start(b_sb[:], b)
+        nc.scalar.dma_start(b1_sb[:], b1)
+        nc.scalar.dma_start(b2_sb[:], b2)
+
+        identity = held.tile([P, P], BF16, name="identity")
+        make_identity(nc, identity[:])
+
+        words_t = held.tile([P, WORDS], BF16, name="words_t")
+        with tc.psum_pool(name="flip_banks", bufs=N_CHUNKS) as flip_banks:
+            for c in range(N_CHUNKS):
+                flipped = flip_banks.tile([P, CHUNK], BF16, name="flipped")
+                for k in range(BLOCKS):
+                    nc.tensor.transpose(flipped[:, k * P : (k + 1) * P], word_rows[c][:, k, :], identity[:])
+                if c % 2 == 0:
+                    nc.vector.tensor_copy(words_t[:, c * CHUNK : (c + 1) * CHUNK], flipped[:])
+                else:
+                    nc.scalar.copy(words_t[:, c * CHUNK : (c + 1) * CHUNK], flipped[:])
+
+        with (
+            tc.psum_pool(name="state_banks", bufs=N_PIECES) as state_banks,
+            tc.psum_pool(name="mlp_banks", bufs=2) as mlp_banks,
+        ):
+            state_ps = []
+            for j in range(N_PIECES):
+                bank = state_banks.tile([P, PIECE], F32, name="state_ps")
+                looked_up = words_t[:].indirect(offsets[:, j * OFFS_COLS : (j + 1) * OFFS_COLS])
+                nc.tensor.matmul(bank[:], w_sb[:], looked_up, start=True, stop=True)
+                state_ps.append(bank)
+
+            state_bf = []
+            for j in range(N_PIECES):
+                rounded = work.tile([P, PIECE], BF16, name="state_bf")
+                nc.vector.tensor_scalar(rounded[:], state_ps[j][:], b_sb[:, 0:1], None, ADD)
+                state_bf.append(rounded)
+
+            for j in range(N_PIECES):
+                state_f32 = work.tile([P, PIECE], F32, name="state_f32")
+                nc.vector.tensor_scalar(state_f32[:], state_ps[j][:], b_sb[:, 0:1], None, ADD)
+                nc.sync.dma_start(out[0:P, j * PIECE : (j + 1) * PIECE], state_f32[:])
+
+            for j in range(N_PIECES):
+                hid_ps = mlp_banks.tile([P, PIECE], F32, name="hid_ps")
+                nc.tensor.matmul(hid_ps[:], w1_sb[:], state_bf[j][:], start=True, stop=True)
+                hid_bf = work.tile([P, PIECE], BF16, name="hid_bf")
+                nc.scalar.activation(hid_bf[:], hid_ps[:], RELU, bias=b1_sb[:, 0:1])
+
+                msg_ps = mlp_banks.tile([P, PIECE], F32, name="msg_ps")
+                nc.tensor.matmul(msg_ps[:], w2_sb[:], hid_bf[:], start=True, stop=True)
+                msg_f32 = work.tile([P, PIECE], F32, name="msg_f32")
+                nc.scalar.activation(msg_f32[:], msg_ps[:], IDENTITY, bias=b2_sb[:, 0:1])
+                nc.sync.dma_start(out[P : 2 * P, j * PIECE : (j + 1) * PIECE], msg_f32[:])

@@ -5,98 +5,122 @@ BF16 = mybir.dt.bfloat16
 F32 = mybir.dt.float32
 U16 = mybir.dt.uint16
 ADD = mybir.AluOpType.add
+MAX = mybir.AluOpType.max
 IDENTITY = mybir.ActivationFunctionType.Identity
 RELU = mybir.ActivationFunctionType.Relu
 
 P = 128
 WORDS = 2048
 NODES = 1024
-PIECE = 256
-N_PIECES = NODES // PIECE
-OFFS_COLS = PIECE // 16
-BLOCKS = 4
-CHUNK = BLOCKS * P
+PER_COLUMN = 16
+
+WIDTHS = [128, 128, 128, 128, 128, 128, 128, 128]
+STARTS = [sum(WIDTHS[:j]) for j in range(len(WIDTHS))]
+N_PIECES = len(WIDTHS)
+assert sum(WIDTHS) == NODES
+
+CHUNK = 512
+PER_PARTITION = CHUNK // P
 N_CHUNKS = WORDS // CHUNK
+
+PSUM_BANKS = 8
+STORE = 256
 
 FLOPS = 3 * 2 * P * P * NODES
 
 
 def tile_gpnn_kernel(tc, table, w, b, w1, b1, w2, b2, offs, out):
     nc = tc.nc
-    table_chunks = table.rearrange("(c k p) d -> c p k d", k=BLOCKS, p=P)
     with (
         tc.tile_pool(name="held", bufs=1) as held,
-        tc.tile_pool(name="rows", bufs=N_CHUNKS) as rows,
-        tc.tile_pool(name="work", bufs=N_PIECES) as work,
+        tc.tile_pool(name="rounded", bufs=N_PIECES) as rounded,
+        tc.psum_pool(name="banks", bufs=PSUM_BANKS) as banks,
     ):
-        word_rows = []
+        chunks = []
         for c in range(N_CHUNKS):
-            chunk = rows.tile([P, BLOCKS, P], BF16, name="word_rows")
-            queue = nc.sync if c % 2 == 0 else nc.scalar
-            queue.dma_start(chunk[:], table_chunks[c])
-            word_rows.append(chunk)
+            chunk = held.tile([P, CHUNK], BF16, name=f"chunk{c}")
+            nc.sync.dma_start(chunk[:], table[c * CHUNK : (c + 1) * CHUNK, :].rearrange("(p a) d -> p (a d)", a=PER_PARTITION))
+            chunks.append(chunk)
 
-        offsets = held.tile([P, NODES // 16], U16, name="offsets")
+        offsets = held.tile([P, NODES // PER_COLUMN], U16, name="offsets")
         nc.sync.dma_start(offsets[:], offs)
 
         w_sb = held.tile([P, P], BF16, name="w_sb")
         w1_sb = held.tile([P, P], BF16, name="w1_sb")
         w2_sb = held.tile([P, P], BF16, name="w2_sb")
-        nc.sync.dma_start(w_sb[:], w)
-        nc.scalar.dma_start(w1_sb[:], w1)
-        nc.scalar.dma_start(w2_sb[:], w2)
-
         b_sb = held.tile([P, 1], F32, name="b_sb")
         b1_sb = held.tile([P, 1], F32, name="b1_sb")
         b2_sb = held.tile([P, 1], F32, name="b2_sb")
+        nc.sync.dma_start(w_sb[:], w)
         nc.sync.dma_start(b_sb[:], b)
-        nc.scalar.dma_start(b1_sb[:], b1)
-        nc.scalar.dma_start(b2_sb[:], b2)
+        nc.sync.dma_start(w1_sb[:], w1)
+        nc.sync.dma_start(b1_sb[:], b1)
+        nc.sync.dma_start(w2_sb[:], w2)
+        nc.sync.dma_start(b2_sb[:], b2)
+
+        zeros = held.tile([P, 1], F32, name="zeros")
+        unused = held.tile([P, 1], F32, name="unused")
+        nc.vector.memset(zeros[:], 0.0)
+        nc.scalar.activation(unused[:], zeros[:], IDENTITY)
 
         identity = held.tile([P, P], BF16, name="identity")
         make_identity(nc, identity[:])
-
         words_t = held.tile([P, WORDS], BF16, name="words_t")
-        with tc.psum_pool(name="flip_banks", bufs=N_CHUNKS) as flip_banks:
-            for c in range(N_CHUNKS):
-                flipped = flip_banks.tile([P, CHUNK], BF16, name="flipped")
-                for k in range(BLOCKS):
-                    nc.tensor.transpose(flipped[:, k * P : (k + 1) * P], word_rows[c][:, k, :], identity[:])
-                if c % 2 == 0:
-                    nc.vector.tensor_copy(words_t[:, c * CHUNK : (c + 1) * CHUNK], flipped[:])
+        for c in range(N_CHUNKS):
+            target = words_t[:, c * CHUNK : (c + 1) * CHUNK].rearrange("d (p a) -> d p a", a=PER_PARTITION)
+            for half in range(2):
+                flipped = banks.tile([P, 2, P], BF16, name="flipped", tag="bank")
+                for i in range(2):
+                    a = 2 * half + i
+                    nc.tensor.transpose(flipped[:, i, :], chunks[c][:, a * P : (a + 1) * P], identity[:])
+                source = flipped[:].rearrange("d i p -> d p i")
+                if half == 0:
+                    nc.vector.tensor_copy(target[:, :, 0:2], source)
                 else:
-                    nc.scalar.copy(words_t[:, c * CHUNK : (c + 1) * CHUNK], flipped[:])
+                    nc.scalar.copy(target[:, :, 2:4], source)
 
-        with (
-            tc.psum_pool(name="state_banks", bufs=N_PIECES) as state_banks,
-            tc.psum_pool(name="mlp_banks", bufs=2) as mlp_banks,
-        ):
-            state_ps = []
-            for j in range(N_PIECES):
-                bank = state_banks.tile([P, PIECE], F32, name="state_ps")
-                looked_up = words_t[:].indirect(offsets[:, j * OFFS_COLS : (j + 1) * OFFS_COLS])
-                nc.tensor.matmul(bank[:], w_sb[:], looked_up, start=True, stop=True)
-                state_ps.append(bank)
+        def add_bias(j, result, bank, bias):
+            if j % 2 == 0:
+                nc.vector.tensor_scalar(result, bank[:], bias[:], None, ADD)
+            else:
+                nc.scalar.activation(result, bank[:], IDENTITY, bias=bias[:])
 
-            state_bf = []
-            for j in range(N_PIECES):
-                rounded = work.tile([P, PIECE], BF16, name="state_bf")
-                nc.vector.tensor_scalar(rounded[:], state_ps[j][:], b_sb[:, 0:1], None, ADD)
-                state_bf.append(rounded)
+        def add_bias_relu(j, result, bank, bias):
+            if j % 2 == 0:
+                nc.vector.tensor_scalar(result, bank[:], bias[:], 0.0, ADD, MAX)
+            else:
+                nc.scalar.activation(result, bank[:], RELU, bias=bias[:])
 
-            for j in range(N_PIECES):
-                state_f32 = work.tile([P, PIECE], F32, name="state_f32")
-                nc.vector.tensor_scalar(state_f32[:], state_ps[j][:], b_sb[:, 0:1], None, ADD)
-                nc.sync.dma_start(out[0:P, j * PIECE : (j + 1) * PIECE], state_f32[:])
 
-            for j in range(N_PIECES):
-                hid_ps = mlp_banks.tile([P, PIECE], F32, name="hid_ps")
-                nc.tensor.matmul(hid_ps[:], w1_sb[:], state_bf[j][:], start=True, stop=True)
-                hid_bf = work.tile([P, PIECE], BF16, name="hid_bf")
-                nc.scalar.activation(hid_bf[:], hid_ps[:], RELU, bias=b1_sb[:, 0:1])
+        state_ps = []
+        for j in range(N_PIECES):
+            bank = banks.tile([P, WIDTHS[j]], F32, name="state_ps", tag="bank")
+            piece_offsets = offsets[:, STARTS[j] // PER_COLUMN : (STARTS[j] + WIDTHS[j]) // PER_COLUMN]
+            nc.tensor.matmul(bank[:], w_sb[:], words_t[:].indirect(piece_offsets), start=True, stop=True)
+            state_ps.append(bank)
 
-                msg_ps = mlp_banks.tile([P, PIECE], F32, name="msg_ps")
-                nc.tensor.matmul(msg_ps[:], w2_sb[:], hid_bf[:], start=True, stop=True)
-                msg_f32 = work.tile([P, PIECE], F32, name="msg_f32")
-                nc.scalar.activation(msg_f32[:], msg_ps[:], IDENTITY, bias=b2_sb[:, 0:1])
-                nc.sync.dma_start(out[P : 2 * P, j * PIECE : (j + 1) * PIECE], msg_f32[:])
+        state_f32 = held.tile([P, NODES], F32, name="state_f32")
+        state_bf = []
+        for j in range(N_PIECES):
+            piece = rounded.tile([P, WIDTHS[j]], BF16, name="state_bf")
+            add_bias(j, piece[:], state_ps[j], b_sb)
+            state_bf.append(piece)
+            add_bias(j, state_f32[:, STARTS[j] : STARTS[j] + WIDTHS[j]], state_ps[j], b_sb)
+        for s in range(0, NODES, STORE):
+            nc.sync.dma_start(out[0:P, s : s + STORE], state_f32[:, s : s + STORE])
+
+        hid_bf = []
+        for j in range(N_PIECES):
+            hid_ps = banks.tile([P, WIDTHS[j]], F32, name="hid_ps", tag="bank")
+            nc.tensor.matmul(hid_ps[:], w1_sb[:], state_bf[j][:], start=True, stop=True)
+            piece = rounded.tile([P, WIDTHS[j]], BF16, name="hid_bf")
+            add_bias_relu(j, piece[:], hid_ps, b1_sb)
+            hid_bf.append(piece)
+
+        msg_f32 = held.tile([P, NODES], F32, name="msg_f32")
+        for j in range(N_PIECES):
+            msg_ps = banks.tile([P, WIDTHS[j]], F32, name="msg_ps", tag="bank")
+            nc.tensor.matmul(msg_ps[:], w2_sb[:], hid_bf[j][:], start=True, stop=True)
+            add_bias(j, msg_f32[:, STARTS[j] : STARTS[j] + WIDTHS[j]], msg_ps, b2_sb)
+        for s in range(0, NODES, STORE):
+            nc.sync.dma_start(out[P : 2 * P, s : s + STORE], msg_f32[:, s : s + STORE])

import concourse.mybir as mybir
from concourse.masks import make_identity

BF16 = mybir.dt.bfloat16
F32 = mybir.dt.float32
U16 = mybir.dt.uint16
ADD = mybir.AluOpType.add
MAX = mybir.AluOpType.max
IDENTITY = mybir.ActivationFunctionType.Identity
RELU = mybir.ActivationFunctionType.Relu

P = 128
WORDS = 2048
NODES = 1024
PER_COLUMN = 16

WIDTHS = [128, 128, 128, 128, 128, 128, 128, 128]
STARTS = [sum(WIDTHS[:j]) for j in range(len(WIDTHS))]
N_PIECES = len(WIDTHS)
assert sum(WIDTHS) == NODES

CHUNK = 512
PER_PARTITION = CHUNK // P
N_CHUNKS = WORDS // CHUNK

PSUM_BANKS = 8
STORE = 256

FLOPS = 3 * 2 * P * P * NODES


def tile_gpnn_kernel(tc, table, w, b, w1, b1, w2, b2, offs, out):
    nc = tc.nc
    with (
        tc.tile_pool(name="held", bufs=1) as held,
        tc.tile_pool(name="rounded", bufs=N_PIECES) as rounded,
        tc.psum_pool(name="banks", bufs=PSUM_BANKS) as banks,
    ):
        chunks = []
        for c in range(N_CHUNKS):
            chunk = held.tile([P, CHUNK], BF16, name=f"chunk{c}")
            nc.sync.dma_start(chunk[:], table[c * CHUNK : (c + 1) * CHUNK, :].rearrange("(p a) d -> p (a d)", a=PER_PARTITION))
            chunks.append(chunk)

        offsets = held.tile([P, NODES // PER_COLUMN], U16, name="offsets")
        nc.sync.dma_start(offsets[:], offs)

        w_sb = held.tile([P, P], BF16, name="w_sb")
        w1_sb = held.tile([P, P], BF16, name="w1_sb")
        w2_sb = held.tile([P, P], BF16, name="w2_sb")
        b_sb = held.tile([P, 1], F32, name="b_sb")
        b1_sb = held.tile([P, 1], F32, name="b1_sb")
        b2_sb = held.tile([P, 1], F32, name="b2_sb")
        nc.sync.dma_start(w_sb[:], w)
        nc.sync.dma_start(b_sb[:], b)
        nc.sync.dma_start(w1_sb[:], w1)
        nc.sync.dma_start(b1_sb[:], b1)
        nc.sync.dma_start(w2_sb[:], w2)
        nc.sync.dma_start(b2_sb[:], b2)

        zeros = held.tile([P, 1], F32, name="zeros")
        unused = held.tile([P, 1], F32, name="unused")
        nc.vector.memset(zeros[:], 0.0)
        nc.scalar.activation(unused[:], zeros[:], IDENTITY)

        identity = held.tile([P, P], BF16, name="identity")
        make_identity(nc, identity[:])
        words_t = held.tile([P, WORDS], BF16, name="words_t")
        for c in range(N_CHUNKS):
            target = words_t[:, c * CHUNK : (c + 1) * CHUNK].rearrange("d (p a) -> d p a", a=PER_PARTITION)
            for half in range(2):
                flipped = banks.tile([P, 2, P], BF16, name="flipped", tag="bank")
                for i in range(2):
                    a = 2 * half + i
                    nc.tensor.transpose(flipped[:, i, :], chunks[c][:, a * P : (a + 1) * P], identity[:])
                source = flipped[:].rearrange("d i p -> d p i")
                if half == 0:
                    nc.vector.tensor_copy(target[:, :, 0:2], source)
                else:
                    nc.scalar.copy(target[:, :, 2:4], source)

        def add_bias(j, result, bank, bias):
            if j % 2 == 0:
                nc.vector.tensor_scalar(result, bank[:], bias[:], None, ADD)
            else:
                nc.scalar.activation(result, bank[:], IDENTITY, bias=bias[:])

        def add_bias_relu(j, result, bank, bias):
            if j % 2 == 0:
                nc.vector.tensor_scalar(result, bank[:], bias[:], 0.0, ADD, MAX)
            else:
                nc.scalar.activation(result, bank[:], RELU, bias=bias[:])


        state_ps = []
        for j in range(N_PIECES):
            bank = banks.tile([P, WIDTHS[j]], F32, name="state_ps", tag="bank")
            piece_offsets = offsets[:, STARTS[j] // PER_COLUMN : (STARTS[j] + WIDTHS[j]) // PER_COLUMN]
            nc.tensor.matmul(bank[:], w_sb[:], words_t[:].indirect(piece_offsets), start=True, stop=True)
            state_ps.append(bank)

        state_f32 = held.tile([P, NODES], F32, name="state_f32")
        state_bf = []
        for j in range(N_PIECES):
            piece = rounded.tile([P, WIDTHS[j]], BF16, name="state_bf")
            add_bias(j, piece[:], state_ps[j], b_sb)
            state_bf.append(piece)
            add_bias(j, state_f32[:, STARTS[j] : STARTS[j] + WIDTHS[j]], state_ps[j], b_sb)
        for s in range(0, NODES, STORE):
            nc.sync.dma_start(out[0:P, s : s + STORE], state_f32[:, s : s + STORE])

        hid_bf = []
        for j in range(N_PIECES):
            hid_ps = banks.tile([P, WIDTHS[j]], F32, name="hid_ps", tag="bank")
            nc.tensor.matmul(hid_ps[:], w1_sb[:], state_bf[j][:], start=True, stop=True)
            piece = rounded.tile([P, WIDTHS[j]], BF16, name="hid_bf")
            add_bias_relu(j, piece[:], hid_ps, b1_sb)
            hid_bf.append(piece)

        msg_f32 = held.tile([P, NODES], F32, name="msg_f32")
        for j in range(N_PIECES):
            msg_ps = banks.tile([P, WIDTHS[j]], F32, name="msg_ps", tag="bank")
            nc.tensor.matmul(msg_ps[:], w2_sb[:], hid_bf[j][:], start=True, stop=True)
            add_bias(j, msg_f32[:, STARTS[j] : STARTS[j] + WIDTHS[j]], msg_ps, b2_sb)
        for s in range(0, NODES, STORE):
            nc.sync.dma_start(out[P : 2 * P, s : s + STORE], msg_f32[:, s : s + STORE])
